import numpy as np
import ml_dtypes


def mxq(x, axis, fmt="e4m3"):
    dtype, down = {"e4m3": (ml_dtypes.float8_e4m3fn, 7), "e5m2": (ml_dtypes.float8_e5m2, 14)}[fmt]
    v = np.moveaxis(np.asarray(x, np.float32).astype(ml_dtypes.bfloat16).astype(np.float64), axis, -1)
    blocks = v.reshape(v.shape[:-1] + (-1, 32))
    amax = np.abs(blocks).max(-1, keepdims=True)
    byte = np.maximum(np.where(amax > 0, np.frexp(amax)[1] - 1 + 127, 0) - down, 1)
    scale = np.exp2(byte - 127.0)
    codes = (blocks / scale).astype(np.float32).astype(dtype).astype(np.float64)
    return np.moveaxis((codes * scale).reshape(v.shape), -1, axis)


WIDE = False


def mx_kscale(k):
    if not WIDE:
        return np.ones(k)
    levels = np.array([10, -10, 5, -5, 0])
    if k % 512:
        return np.exp2(np.random.permutation(np.resize(levels, k // 32))).repeat(32)
    a = np.empty((k // 512, 16))
    for p in range(k // 512):
        a[p, :8] = np.random.permutation(np.resize(levels, 8))
        for g in range(8):
            far = levels[np.abs(levels - a[p, g]) >= 10]
            a[p, g + 8] = far[np.random.randint(len(far))]
    return np.exp2(a.ravel()).repeat(32)


BF16 = ml_dtypes.bfloat16


def bf(x):
    return np.asarray(x, np.float32).astype(BF16)


def f64(x):
    return np.asarray(x).astype(np.float64)


B, S, E, H, D = 8, 512, 512, 1, 512


def setup_inputs():
    s = mx_kscale(E)
    ckv = 0.75 * D ** 0.25 / np.sqrt(E)
    cq = 3.0 / np.sqrt(E)
    return {"x": bf(np.random.standard_normal((B, S, E)) * s),
            "Wq": bf(np.random.standard_normal((E, H * D)) * cq / s[:, None]),
            "bq": bf(np.random.standard_normal(H * D) * 0.25),
            "Wk": bf(np.random.standard_normal((E, H * D)) * ckv / s[:, None]),
            "bk": bf(np.random.standard_normal(H * D)),
            "Wv": bf(np.random.standard_normal((E, H * D)) * ckv / s[:, None]),
            "bv": bf(np.random.standard_normal(H * D))}


def reference(x, Wq, bq, Wk, bk, Wv, bv):
    xq = mxq(f64(x), 2, "e4m3")

    def proj(W, bias):
        y = (xq @ mxq(f64(W), 0, "e4m3")) + f64(bias)
        return y.reshape(B, S, H, D).transpose(0, 2, 1, 3)

    q = proj(Wq, bq)
    k = proj(Wk, bk)
    v = proj(Wv, bv)
    kv = k * np.swapaxes(v, -1, -2) * (1.0 / np.sqrt(D))
    e = np.exp(kv - kv.max(axis=2, keepdims=True))
    attn = e / e.sum(axis=2, keepdims=True)
    return np.sum(attn * q, axis=2)

@@ -1,0 +1,259 @@
+import math
+
+import concourse.mybir as mybir
+from concourse.masks import make_identity
+
+F32 = mybir.dt.float32
+BF16 = mybir.dt.bfloat16
+U32 = mybir.dt.uint32
+U8 = mybir.dt.uint8
+FP8X4 = mybir.dt.float8_e4m3fn_x4
+ALU = mybir.AluOpType
+ACT = mybir.ActivationFunctionType
+
+B = 8
+S = 512
+E = 512
+D = 512
+P = 128
+PACK = 4
+BLOCKS = S // P
+TILES = B * BLOCKS
+HALF_S = S // 2
+LAG_K = 1
+LAG_SCORE = 2
+LAG_Q = 4
+
+FLOPS = 2 * B * S * E * 3 * D
+
+
+def tile_multihead_attention_pa_t_kernel(tc, x, Wq, bq, Wk, bk, Wv, bv, out):
+    nc = tc.nc
+    inv_sqrt_d = 1.0 / math.sqrt(D)
+
+    with tc.tile_pool(name="const", bufs=1) as const, tc.tile_pool(
+        name="xin", bufs=B
+    ) as xin, tc.tile_pool(name="xq", bufs=3) as xq, tc.tile_pool(
+        name="work", bufs=4
+    ) as work, tc.psum_pool(name="ps_misc", bufs=2) as ps_misc, tc.psum_pool(
+        name="ps_proj", bufs=2
+    ) as ps_proj, tc.manual_schedule():
+        bias_in = const.tile([2 * BLOCKS, P], BF16, name="bias_in")
+        nc.scalar.dma_start(out=bias_in[0:BLOCKS, :], in_=bk.rearrange("(r c) -> r c", c=P))
+        nc.scalar.dma_start(out=bias_in[BLOCKS : 2 * BLOCKS, :], in_=bq.rearrange("(r c) -> r c", c=P))
+        bv_in = const.tile([1, D], BF16, name="bv_in")
+        nc.scalar.dma_start(out=bv_in[:], in_=bv.rearrange("(o n) -> o n", o=1))
+
+        x_rows = {}
+
+        def load_x(b, h):
+            if h == 0:
+                x_rows[b] = xin.tile([P, BLOCKS * E], BF16, name="x_rows")
+            nc.sync.dma_start(
+                out=x_rows[b][:, h * 2 * E : (h + 1) * 2 * E].rearrange("p (r e) -> p r e", r=2),
+                in_=x[b, h * HALF_S : (h + 1) * HALF_S, :].rearrange("(r p) e -> p r e", p=P),
+            )
+
+        def load_weight(w, name):
+            raw = const.tile([P, PACK, D], BF16, name=name + "_raw")
+            nc.sync.dma_start(
+                out=raw[:].rearrange("p t n -> p (t n)"),
+                in_=w.rearrange("(p t) n -> p (t n)", t=PACK),
+            )
+            return raw
+
+        load_x(0, 0)
+        wv_raw = load_weight(Wv, "wv")
+        load_x(0, 1)
+        wk_raw = load_weight(Wk, "wk")
+        wq_raw = load_weight(Wq, "wq")
+        for b in range(1, B):
+            load_x(b, 0)
+            load_x(b, 1)
+
+        ident = const.tile([P, P], F32, name="ident")
+        make_identity(nc, ident[:])
+        zero_col = const.tile([P, 1], F32, name="zero_col")
+        nc.vector.memset(zero_col[:], 0.0)
+        one_col = const.tile([P, 1], F32, name="one_col")
+        nc.scalar.activation(out=one_col[:], in_=zero_col[:], func=ACT.Exp)
+        ones = const.tile([P, P], BF16, name="ones")
+        nc.vector.memset(ones[:], 1.0)
+        bias_rows = const.tile([P, P], F32, name="bias_rows")
+        nc.vector.memset(bias_rows[:], 0.0)
+        bv_row = const.tile([P, D], BF16, name="bv_row")
+        nc.vector.memset(bv_row[:], 0.0)
+        result = const.tile([P, P], F32, name="result")
+        nc.vector.memset(result[:], 0.0)
+        neg_max = const.tile([P, TILES], F32, name="neg_max")
+        denom = const.tile([P, TILES], F32, name="denom")
+        numer = const.tile([P, TILES], F32, name="numer")
+
+        x_grouped = {}
+        x_mx = {}
+
+        def turn_x(b, h):
+            if h == 0:
+                x_grouped[b] = xq.tile([P, S * PACK], BF16, name="x_grouped", align_bytes=64)
+            words = x_rows[b][:].bitcast(F32)
+            xt = ps_misc.tile([P, 2, 2, P], F32, tag="misc", name="xt")
+            for r in range(2):
+                for u in range(2):
+                    first = (2 * h + r) * (E // 2)
+                    nc.tensor.transpose(
+                        xt[:, r, u, :], words[:, first + u : first + E // 2 : 2], ident[:]
+                    )
+            nc.scalar.copy(
+                out=x_grouped[b][:, h * HALF_S * PACK : (h + 1) * HALF_S * PACK]
+                .bitcast(F32)
+                .rearrange("p (r i u) -> p r i u", r=2, u=2),
+                in_=xt[:].rearrange("p r u i -> p r i u"),
+            )
+
+        def quantise_x(b):
+            codes = xq.tile([P, S], U32, name="x_codes", align_bytes=64)
+            scales = xq.tile([P, S], U8, name="x_scales", align_bytes=64)
+            nc.vector.quantize_mx(out=codes[:].bitcast(FP8X4), scales=scales[:], in_=x_grouped[b][:])
+            x_mx[b] = (codes, scales)
+
+        w_grouped = {}
+        w_mx = {}
+
+        def regroup_weight(raw, name):
+            w_grouped[name] = const.tile([P, D, PACK], BF16, name=name + "_grouped", align_bytes=64)
+            nc.vector.tensor_copy(
+                out=w_grouped[name][:].rearrange("p (c i) t -> p c t i", i=4),
+                in_=raw[:].rearrange("p t (c i) -> p c t i", i=4),
+            )
+
+        def quantise_weight(name):
+            codes = const.tile([P, D], U32, name=name + "_codes", align_bytes=64)
+            scales = const.tile([P, D], U8, name=name + "_scales", align_bytes=64)
+            nc.vector.quantize_mx(
+                out=codes[:].bitcast(FP8X4),
+                scales=scales[:],
+                in_=w_grouped[name][:].rearrange("p n t -> p (n t)"),
+            )
+            w_mx[name] = (codes, scales)
+
+        turn_x(0, 0)
+        nc.vector.tensor_copy(out=bias_rows[0 : 2 * BLOCKS, :], in_=bias_in[:])
+        bias_ps = ps_misc.tile([P, P], F32, tag="misc", name="bias_ps")
+        nc.tensor.transpose(bias_ps[:], bias_rows[:], ident[:])
+        bias_cols = const.tile([P, 2 * BLOCKS], F32, name="bias_cols")
+        nc.vector.tensor_copy(out=bias_cols[:], in_=bias_ps[:, 0 : 2 * BLOCKS])
+        nc.vector.tensor_copy(out=bv_row[0:1, :], in_=bv_in[:])
+        bv_ps = ps_misc.tile([P, D], F32, tag="misc", name="bv_ps")
+        nc.tensor.matmul(bv_ps[:], lhsT=ones[:], rhs=bv_row[:], start=True, stop=True)
+        bv_all = const.tile([P, D], F32, name="bv_all")
+        nc.scalar.mul(out=bv_all[:], in_=bv_ps[:], mul=inv_sqrt_d)
+        turn_x(0, 1)
+
+        regroup_weight(wv_raw, "wv")
+        quantise_weight("wv")
+        quantise_x(0)
+        regroup_weight(wk_raw, "wk")
+        quantise_weight("wk")
+
+        def project(lhs, lhs_cols, rhs, tag):
+            acc = ps_proj.tile([P, S], F32, tag=tag, name=tag + "_ps")
+            nc.tensor.matmul_mx(
+                out=acc[:],
+                lhsT=lhs[0][:, lhs_cols].bitcast(FP8X4),
+                lhsT_scale=lhs[1][:, lhs_cols],
+                rhs=rhs[0][:].bitcast(FP8X4),
+                rhs_scale=rhs[1][:],
+                start=True,
+                stop=True,
+            )
+            return acc
+
+        def block_cols(t):
+            return slice((t % BLOCKS) * P, (t % BLOCKS + 1) * P)
+
+        v_biased = {}
+        k_ps = {}
+        score = {}
+        weight = {}
+
+        def stage_v(t):
+            v_ps = project(x_mx[t // BLOCKS], block_cols(t), w_mx["wv"], "v")
+            v_sb = work.tile([P, S], F32, name="v_sb")
+            nc.scalar.mul(out=v_sb[:], in_=v_ps[:], mul=inv_sqrt_d)
+            v_biased[t] = work.tile([P, S], F32, name="v_biased")
+            nc.gpsimd.tensor_tensor(out=v_biased[t][:], in0=v_sb[:], in1=bv_all[:], op=ALU.add)
+
+        def stage_k(t):
+            k_ps[t] = project(w_mx["wk"], block_cols(t), x_mx[t // BLOCKS], "k")
+
+        def stage_score(t):
+            score[t] = work.tile([P, S], F32, name="score")
+            nc.vector.scalar_tensor_tensor(
+                out=score[t][:],
+                in0=k_ps[t][:],
+                scalar=bias_cols[:, t % BLOCKS : t % BLOCKS + 1],
+                in1=v_biased[t][:],
+                op0=ALU.add,
+                op1=ALU.mult,
+            )
+
+        def stage_softmax(t):
+            nc.vector.tensor_reduce(
+                out=neg_max[:, t : t + 1],
+                in_=score[t][:],
+                axis=mybir.AxisListType.X,
+                op=ALU.max,
+                negate=True,
+            )
+            weight[t] = work.tile([P, S], F32, name="weight")
+            nc.scalar.activation(
+                out=weight[t][:],
+                in_=score[t][:],
+                func=ACT.Exp,
+                bias=neg_max[:, t : t + 1],
+                scale=1.0,
+                accum_out=denom[:, t : t + 1],
+            )
+
+        def stage_q(t):
+            q_ps = project(w_mx["wq"], block_cols(t), x_mx[t // BLOCKS], "q")
+            weighted = work.tile([P, S], F32, name="weighted")
+            nc.vector.scalar_tensor_tensor(
+                out=weighted[:],
+                in0=q_ps[:],
+                scalar=bias_cols[:, BLOCKS + t % BLOCKS : BLOCKS + t % BLOCKS + 1],
+                in1=weight[t][:],
+                op0=ALU.add,
+                op1=ALU.mult,
+                accum_out=numer[:, t : t + 1],
+            )
+
+        for step in range(TILES + LAG_Q):
+            if step < TILES:
+                stage_v(step)
+            if 0 <= step - LAG_K < TILES:
+                stage_k(step - LAG_K)
+            if 0 <= step - LAG_SCORE < TILES:
+                stage_score(step - LAG_SCORE)
+            if 0 <= step - LAG_Q:
+                stage_q(step - LAG_Q)
+            if step == LAG_Q - 2:
+                regroup_weight(wq_raw, "wq")
+            if step == LAG_Q - 1:
+                quantise_weight("wq")
+            if 0 <= step - LAG_SCORE < TILES:
+                stage_softmax(step - LAG_SCORE)
+            next_b = step // BLOCKS + 1
+            if next_b < B and step % BLOCKS < 2:
+                turn_x(next_b, step % BLOCKS)
+            if next_b < B and step % BLOCKS == 2:
+                quantise_x(next_b)
+
+        inv_denom = const.tile([P, TILES], F32, name="inv_denom")
+        nc.vector.reciprocal(out=inv_denom[:], in_=denom[:])
+        nc.vector.tensor_mul(out=result[:, 0:TILES], in0=numer[:], in1=inv_denom[:])
+        result_ps = ps_misc.tile([P, P], F32, tag="misc", name="result_ps")
+        nc.tensor.transpose(result_ps[:], result[:], ident[:])
+        result_rows = const.tile([TILES, P], F32, name="result_rows")
+        nc.scalar.copy(out=result_rows[:], in_=result_ps[0:TILES, :])
+        nc.sync.dma_start(out=out.rearrange("b h (r p) -> (b h r) p", p=P), in_=result_rows[:])

@@ -22,7 +22,8 @@ TILES = B * BLOCKS
 HALF_S = S // 2
 LAG_K = 1
 LAG_SCORE = 2
-LAG_Q = 4
+LAG_MAX = 2
+LAG_Q = 5
 
 FLOPS = 2 * B * S * E * 3 * D
 
@@ -88,6 +89,7 @@ def tile_multihead_attention_pa_t_kernel(tc, x, Wq, bq, Wk, bk, Wv, bv, out):
         neg_max = const.tile([P, TILES], F32, name="neg_max")
         denom = const.tile([P, TILES], F32, name="denom")
         numer = const.tile([P, TILES], F32, name="numer")
+        inv_denom = const.tile([P, TILES], F32, name="inv_denom")
 
         x_grouped = {}
         x_mx = {}
@@ -110,50 +112,60 @@ def tile_multihead_attention_pa_t_kernel(tc, x, Wq, bq, Wk, bk, Wv, bv, out):
                 in_=xt[:].rearrange("p r u i -> p r i u"),
             )
 
-        def quantise_x(b):
-            codes = xq.tile([P, S], U32, name="x_codes", align_bytes=64)
-            scales = xq.tile([P, S], U8, name="x_scales", align_bytes=64)
-            nc.vector.quantize_mx(out=codes[:].bitcast(FP8X4), scales=scales[:], in_=x_grouped[b][:])
-            x_mx[b] = (codes, scales)
+        def quantise_x(b, c0=0, c1=S):
+            if c0 == 0:
+                x_mx[b] = (
+                    xq.tile([P, S], U32, name="x_codes", align_bytes=64),
+                    xq.tile([P, S], U8, name="x_scales", align_bytes=64),
+                )
+            codes, scales = x_mx[b]
+            nc.vector.quantize_mx(
+                out=codes[:, c0:c1].bitcast(FP8X4),
+                scales=scales[:, c0:c1],
+                in_=x_grouped[b][:, c0 * PACK : c1 * PACK],
+            )
 
         w_grouped = {}
         w_mx = {}
-
-        def regroup_weight(raw, name):
+        for name in ("wv", "wk", "wq"):
             w_grouped[name] = const.tile([P, D, PACK], BF16, name=name + "_grouped", align_bytes=64)
-            nc.vector.tensor_copy(
-                out=w_grouped[name][:].rearrange("p (c i) t -> p c t i", i=4),
-                in_=raw[:].rearrange("p t (c i) -> p c t i", i=4),
+            w_mx[name] = (
+                const.tile([P, D], U32, name=name + "_codes", align_bytes=64),
+                const.tile([P, D], U8, name=name + "_scales", align_bytes=64),
             )
 
-        def quantise_weight(name):
-            codes = const.tile([P, D], U32, name=name + "_codes", align_bytes=64)
-            scales = const.tile([P, D], U8, name=name + "_scales", align_bytes=64)
-            nc.vector.quantize_mx(
-                out=codes[:].bitcast(FP8X4),
-                scales=scales[:],
-                in_=w_grouped[name][:].rearrange("p n t -> p (n t)"),
+        def regroup_weight(copy, raw, name, c0, c1):
+            copy(
+                out=w_grouped[name][:, c0:c1, :].rearrange("p (c i) t -> p c t i", i=4),
+                in_=raw[:, :, c0:c1].rearrange("p t (c i) -> p c t i", i=4),
             )
-            w_mx[name] = (codes, scales)
+
+        def quantise_weight(name, c0, c1):
+            codes, scales = w_mx[name]
+            nc.vector.quantize_mx(
+                out=codes[:, c0:c1].bitcast(FP8X4),
+                scales=scales[:, c0:c1],
+                in_=w_grouped[name][:].rearrange("p n t -> p (n t)")[:, c0 * PACK : c1 * PACK],
+            )
 
         turn_x(0, 0)
-        nc.vector.tensor_copy(out=bias_rows[0 : 2 * BLOCKS, :], in_=bias_in[:])
+        turn_x(0, 1)
+        nc.gpsimd.tensor_copy(out=bias_rows[0 : 2 * BLOCKS, :], in_=bias_in[:])
         bias_ps = ps_misc.tile([P, P], F32, tag="misc", name="bias_ps")
         nc.tensor.transpose(bias_ps[:], bias_rows[:], ident[:])
-        bias_cols = const.tile([P, 2 * BLOCKS], F32, name="bias_cols")
-        nc.vector.tensor_copy(out=bias_cols[:], in_=bias_ps[:, 0 : 2 * BLOCKS])
-        nc.vector.tensor_copy(out=bv_row[0:1, :], in_=bv_in[:])
+        nc.gpsimd.tensor_copy(out=bv_row[0:1, :], in_=bv_in[:])
         bv_ps = ps_misc.tile([P, D], F32, tag="misc", name="bv_ps")
         nc.tensor.matmul(bv_ps[:], lhsT=ones[:], rhs=bv_row[:], start=True, stop=True)
+
+        regroup_weight(nc.vector.tensor_copy, wv_raw, "wv", 0, D)
+        quantise_weight("wv", 0, D)
+        regroup_weight(nc.scalar.copy, wk_raw, "wk", 0, P)
+        quantise_x(0)
+        bias_cols = const.tile([P, 2 * BLOCKS], F32, name="bias_cols")
+        nc.scalar.copy(out=bias_cols[:], in_=bias_ps[:, 0 : 2 * BLOCKS])
         bv_all = const.tile([P, D], F32, name="bv_all")
         nc.scalar.mul(out=bv_all[:], in_=bv_ps[:], mul=inv_sqrt_d)
-        turn_x(0, 1)
-
-        regroup_weight(wv_raw, "wv")
-        quantise_weight("wv")
-        quantise_x(0)
-        regroup_weight(wk_raw, "wk")
-        quantise_weight("wk")
+        quantise_weight("wk", 0, P)
 
         def project(lhs, lhs_cols, rhs, tag):
             acc = ps_proj.tile([P, S], F32, tag=tag, name=tag + "_ps")
@@ -171,6 +183,9 @@ def tile_multihead_attention_pa_t_kernel(tc, x, Wq, bq, Wk, bk, Wv, bv, out):
         def block_cols(t):
             return slice((t % BLOCKS) * P, (t % BLOCKS + 1) * P)
 
+        def on_gpsimd(t):
+            return False
+
         v_biased = {}
         k_ps = {}
         score = {}
@@ -178,13 +193,38 @@ def tile_multihead_attention_pa_t_kernel(tc, x, Wq, bq, Wk, bk, Wv, bv, out):
 
         def stage_v(t):
             v_ps = project(x_mx[t // BLOCKS], block_cols(t), w_mx["wv"], "v")
-            v_sb = work.tile([P, S], F32, name="v_sb")
-            nc.scalar.mul(out=v_sb[:], in_=v_ps[:], mul=inv_sqrt_d)
             v_biased[t] = work.tile([P, S], F32, name="v_biased")
-            nc.gpsimd.tensor_tensor(out=v_biased[t][:], in0=v_sb[:], in1=bv_all[:], op=ALU.add)
+            if t < 1:
+                nc.vector.scalar_tensor_tensor(
+                    out=v_biased[t][:],
+                    in0=v_ps[:],
+                    scalar=inv_sqrt_d,
+                    in1=bv_all[:],
+                    op0=ALU.mult,
+                    op1=ALU.add,
+                )
+            else:
+                v_sb = work.tile([P, S], F32, name="v_sb")
+                nc.scalar.mul(out=v_sb[:], in_=v_ps[:], mul=inv_sqrt_d)
+                nc.gpsimd.tensor_tensor(out=v_biased[t][:], in0=v_sb[:], in1=bv_all[:], op=ALU.add)
 
         def stage_k(t):
             k_ps[t] = project(w_mx["wk"], block_cols(t), x_mx[t // BLOCKS], "k")
+
+        def stage_score_gpsimd(t):
+            stage_k(t)
+            k_biased = work.tile([P, S], F32, name="k_biased")
+            nc.scalar.activation(
+                out=k_biased[:],
+                in_=k_ps[t][:],
+                func=ACT.Identity,
+                bias=bias_cols[:, t % BLOCKS : t % BLOCKS + 1],
+                scale=1.0,
+            )
+            score[t] = work.tile([P, S], F32, name="score")
+            nc.gpsimd.tensor_tensor(
+                out=score[t][:], in0=k_biased[:], in1=v_biased[t][:], op=ALU.mult
+            )
 
         def stage_score(t):
             score[t] = work.tile([P, S], F32, name="score")
@@ -197,7 +237,7 @@ def tile_multihead_attention_pa_t_kernel(tc, x, Wq, bq, Wk, bk, Wv, bv, out):
                 op1=ALU.mult,
             )
 
-        def stage_softmax(t):
+        def stage_max(t):
             nc.vector.tensor_reduce(
                 out=neg_max[:, t : t + 1],
                 in_=score[t][:],
@@ -205,6 +245,8 @@ def tile_multihead_attention_pa_t_kernel(tc, x, Wq, bq, Wk, bk, Wv, bv, out):
                 op=ALU.max,
                 negate=True,
             )
+
+        def stage_exp(t):
             weight[t] = work.tile([P, S], F32, name="weight")
             nc.scalar.activation(
                 out=weight[t][:],
@@ -228,29 +270,43 @@ def tile_multihead_attention_pa_t_kernel(tc, x, Wq, bq, Wk, bk, Wv, bv, out):
                 accum_out=numer[:, t : t + 1],
             )
 
+        def in_range(t):
+            return 0 <= t < TILES
+
+        late_weights = {
+            2: (wk_raw, "wk", P, 2 * P),
+            3: (wk_raw, "wk", 2 * P, D),
+            4: (wq_raw, "wq", 0, 2 * P),
+            5: (wq_raw, "wq", 2 * P, D),
+        }
         for step in range(TILES + LAG_Q):
             if step < TILES:
                 stage_v(step)
-            if 0 <= step - LAG_K < TILES:
-                stage_k(step - LAG_K)
-            if 0 <= step - LAG_SCORE < TILES:
+            if step < TILES and on_gpsimd(step):
+                stage_score_gpsimd(step)
+            if in_range(step - LAG_SCORE) and not on_gpsimd(step - LAG_SCORE):
                 stage_score(step - LAG_SCORE)
-            if 0 <= step - LAG_Q:
+            if step in late_weights:
+                regroup_weight(nc.vector.tensor_copy, *late_weights[step])
+            if in_range(step - LAG_Q):
+                if step - LAG_Q == TILES - 1:
+                    nc.vector.reciprocal(out=inv_denom[:], in_=denom[:])
                 stage_q(step - LAG_Q)
-            if step == LAG_Q - 2:
-                regroup_weight(wq_raw, "wq")
-            if step == LAG_Q - 1:
-                quantise_weight("wq")
-            if 0 <= step - LAG_SCORE < TILES:
-                stage_softmax(step - LAG_SCORE)
+            if in_range(step - LAG_MAX):
+                stage_max(step - LAG_MAX)
+            if step in late_weights:
+                quantise_weight(*late_weights[step][1:])
+            if in_range(step - LAG_K) and not on_gpsimd(step - LAG_K):
+                stage_k(step - LAG_K)
             next_b = step // BLOCKS + 1
-            if next_b < B and step % BLOCKS < 2:
-                turn_x(next_b, step % BLOCKS)
             if next_b < B and step % BLOCKS == 2:
                 quantise_x(next_b)
+            if in_range(step - LAG_MAX):
+                stage_exp(step - LAG_MAX)
+            if next_b < B and step % BLOCKS < 2:
+                turn_x(next_b, step % BLOCKS)
 
-        inv_denom = const.tile([P, TILES], F32, name="inv_denom")
-        nc.vector.reciprocal(out=inv_denom[:], in_=denom[:])
+
         nc.vector.tensor_mul(out=result[:, 0:TILES], in0=numer[:], in1=inv_denom[:])
         result_ps = ps_misc.tile([P, P], F32, tag="misc", name="result_ps")
         nc.tensor.transpose(result_ps[:], result[:], ident[:])

@@ -22,7 +22,7 @@ TILES = B * BLOCKS
 HALF_S = S // 2
 LAG_K = 1
 LAG_SCORE = 2
-LAG_MAX = 2
+LAG_MAX = 3
 LAG_Q = 5
 
 FLOPS = 2 * B * S * E * 3 * D
@@ -184,7 +184,7 @@ def tile_multihead_attention_pa_t_kernel(tc, x, Wq, bq, Wk, bk, Wv, bv, out):
             return slice((t % BLOCKS) * P, (t % BLOCKS + 1) * P)
 
         def on_gpsimd(t):
-            return False
+            return t % BLOCKS == BLOCKS - 1
 
         v_biased = {}
         k_ps = {}
@@ -282,20 +282,20 @@ def tile_multihead_attention_pa_t_kernel(tc, x, Wq, bq, Wk, bk, Wv, bv, out):
         for step in range(TILES + LAG_Q):
             if step < TILES:
                 stage_v(step)
-            if step < TILES and on_gpsimd(step):
-                stage_score_gpsimd(step)
             if in_range(step - LAG_SCORE) and not on_gpsimd(step - LAG_SCORE):
                 stage_score(step - LAG_SCORE)
             if step in late_weights:
                 regroup_weight(nc.vector.tensor_copy, *late_weights[step])
+            if in_range(step - LAG_MAX):
+                stage_max(step - LAG_MAX)
             if in_range(step - LAG_Q):
                 if step - LAG_Q == TILES - 1:
                     nc.vector.reciprocal(out=inv_denom[:], in_=denom[:])
                 stage_q(step - LAG_Q)
-            if in_range(step - LAG_MAX):
-                stage_max(step - LAG_MAX)
             if step in late_weights:
                 quantise_weight(*late_weights[step][1:])
+            if step < TILES and on_gpsimd(step):
+                stage_score_gpsimd(step)
             if in_range(step - LAG_K) and not on_gpsimd(step - LAG_K):
                 stage_k(step - LAG_K)
             next_b = step // BLOCKS + 1

@@ -23,6 +23,8 @@ HALF_S = S // 2
 LAG_K = 1
 LAG_SCORE = 2
 LAG_MAX = 3
+LAG_EXP = 3
+FUSED = 4
 LAG_Q = 5
 
 FLOPS = 2 * B * S * E * 3 * D
@@ -35,7 +37,7 @@ def tile_multihead_attention_pa_t_kernel(tc, x, Wq, bq, Wk, bk, Wv, bv, out):
     with tc.tile_pool(name="const", bufs=1) as const, tc.tile_pool(
         name="xin", bufs=B
     ) as xin, tc.tile_pool(name="xq", bufs=3) as xq, tc.tile_pool(
-        name="work", bufs=4
+        name="work", bufs=6
     ) as work, tc.psum_pool(name="ps_misc", bufs=2) as ps_misc, tc.psum_pool(
         name="ps_proj", bufs=2
     ) as ps_proj, tc.manual_schedule():
@@ -63,12 +65,14 @@ def tile_multihead_attention_pa_t_kernel(tc, x, Wq, bq, Wk, bk, Wv, bv, out):
             )
             return raw
 
-        load_x(0, 0)
         wv_raw = load_weight(Wv, "wv")
+        load_x(0, 0)
         load_x(0, 1)
         wk_raw = load_weight(Wk, "wk")
+        load_x(1, 0)
+        load_x(1, 1)
         wq_raw = load_weight(Wq, "wq")
-        for b in range(1, B):
+        for b in range(2, B):
             load_x(b, 0)
             load_x(b, 1)
 
@@ -94,9 +98,9 @@ def tile_multihead_attention_pa_t_kernel(tc, x, Wq, bq, Wk, bk, Wv, bv, out):
         x_grouped = {}
         x_mx = {}
 
+        x_turned = {}
+
         def turn_x(b, h):
-            if h == 0:
-                x_grouped[b] = xq.tile([P, S * PACK], BF16, name="x_grouped", align_bytes=64)
             words = x_rows[b][:].bitcast(F32)
             xt = ps_misc.tile([P, 2, 2, P], F32, tag="misc", name="xt")
             for r in range(2):
@@ -105,11 +109,16 @@ def tile_multihead_attention_pa_t_kernel(tc, x, Wq, bq, Wk, bk, Wv, bv, out):
                     nc.tensor.transpose(
                         xt[:, r, u, :], words[:, first + u : first + E // 2 : 2], ident[:]
                     )
+            x_turned[b, h] = xt
+
+        def group_x(b, h):
+            if h == 0:
+                x_grouped[b] = xq.tile([P, S * PACK], BF16, name="x_grouped", align_bytes=64)
             nc.scalar.copy(
                 out=x_grouped[b][:, h * HALF_S * PACK : (h + 1) * HALF_S * PACK]
                 .bitcast(F32)
                 .rearrange("p (r i u) -> p r i u", r=2, u=2),
-                in_=xt[:].rearrange("p r u i -> p r i u"),
+                in_=x_turned[b, h][:].rearrange("p r u i -> p r i u"),
             )
 
         def quantise_x(b, c0=0, c1=S):
@@ -150,21 +159,25 @@ def tile_multihead_attention_pa_t_kernel(tc, x, Wq, bq, Wk, bk, Wv, bv, out):
 
         turn_x(0, 0)
         turn_x(0, 1)
-        nc.gpsimd.tensor_copy(out=bias_rows[0 : 2 * BLOCKS, :], in_=bias_in[:])
+        regroup_weight(nc.scalar.copy, wv_raw, "wv", 0, 128)
+        group_x(0, 0)
+        group_x(0, 1)
+        regroup_weight(nc.vector.tensor_copy, wv_raw, "wv", 128, 512)
+        nc.vector.tensor_copy(out=bias_rows[0 : 2 * BLOCKS, :], in_=bias_in[:])
         bias_ps = ps_misc.tile([P, P], F32, tag="misc", name="bias_ps")
         nc.tensor.transpose(bias_ps[:], bias_rows[:], ident[:])
-        nc.gpsimd.tensor_copy(out=bv_row[0:1, :], in_=bv_in[:])
+        nc.vector.tensor_copy(out=bv_row[0:1, :], in_=bv_in[:])
         bv_ps = ps_misc.tile([P, D], F32, tag="misc", name="bv_ps")
         nc.tensor.matmul(bv_ps[:], lhsT=ones[:], rhs=bv_row[:], start=True, stop=True)
-
-        regroup_weight(nc.vector.tensor_copy, wv_raw, "wv", 0, D)
-        quantise_weight("wv", 0, D)
-        regroup_weight(nc.scalar.copy, wk_raw, "wk", 0, P)
-        quantise_x(0)
-        bias_cols = const.tile([P, 2 * BLOCKS], F32, name="bias_cols")
-        nc.scalar.copy(out=bias_cols[:], in_=bias_ps[:, 0 : 2 * BLOCKS])
+        regroup_weight(nc.scalar.copy, wk_raw, "wk", 0, 128)
         bv_all = const.tile([P, D], F32, name="bv_all")
         nc.scalar.mul(out=bv_all[:], in_=bv_ps[:], mul=inv_sqrt_d)
+        bias_cols = const.tile([P, 2 * BLOCKS], F32, name="bias_cols")
+        nc.scalar.copy(out=bias_cols[:], in_=bias_ps[:, 0 : 2 * BLOCKS])
+        regroup_weight(nc.scalar.copy, wk_raw, "wk", 128, 256)
+        quantise_weight("wv", 0, D)
+        quantise_x(0)
+        regroup_weight(nc.vector.tensor_copy, wk_raw, "wk", 256, 512)
         quantise_weight("wk", 0, P)
 
         def project(lhs, lhs_cols, rhs, tag):
@@ -184,7 +197,7 @@ def tile_multihead_attention_pa_t_kernel(tc, x, Wq, bq, Wk, bk, Wv, bv, out):
             return slice((t % BLOCKS) * P, (t % BLOCKS + 1) * P)
 
         def on_gpsimd(t):
-            return t % BLOCKS == BLOCKS - 1
+            return t % BLOCKS == BLOCKS - 1 and t >= BLOCKS
 
         v_biased = {}
         k_ps = {}
@@ -194,7 +207,7 @@ def tile_multihead_attention_pa_t_kernel(tc, x, Wq, bq, Wk, bk, Wv, bv, out):
         def stage_v(t):
             v_ps = project(x_mx[t // BLOCKS], block_cols(t), w_mx["wv"], "v")
             v_biased[t] = work.tile([P, S], F32, name="v_biased")
-            if t < 1:
+            if t < FUSED:
                 nc.vector.scalar_tensor_tensor(
                     out=v_biased[t][:],
                     in0=v_ps[:],
@@ -211,19 +224,23 @@ def tile_multihead_attention_pa_t_kernel(tc, x, Wq, bq, Wk, bk, Wv, bv, out):
         def stage_k(t):
             k_ps[t] = project(w_mx["wk"], block_cols(t), x_mx[t // BLOCKS], "k")
 
-        def stage_score_gpsimd(t):
+        k_biased = {}
+
+        def empty_k(t):
             stage_k(t)
-            k_biased = work.tile([P, S], F32, name="k_biased")
+            k_biased[t] = work.tile([P, S], F32, name="k_biased")
             nc.scalar.activation(
-                out=k_biased[:],
+                out=k_biased[t][:],
                 in_=k_ps[t][:],
                 func=ACT.Identity,
                 bias=bias_cols[:, t % BLOCKS : t % BLOCKS + 1],
                 scale=1.0,
             )
+
+        def stage_score_gpsimd(t):
             score[t] = work.tile([P, S], F32, name="score")
             nc.gpsimd.tensor_tensor(
-                out=score[t][:], in0=k_biased[:], in1=v_biased[t][:], op=ALU.mult
+                out=score[t][:], in0=k_biased[t][:], in1=v_biased[t][:], op=ALU.mult
             )
 
         def stage_score(t):
@@ -273,39 +290,53 @@ def tile_multihead_attention_pa_t_kernel(tc, x, Wq, bq, Wk, bk, Wv, bv, out):
         def in_range(t):
             return 0 <= t < TILES
 
-        late_weights = {
-            2: (wk_raw, "wk", P, 2 * P),
-            3: (wk_raw, "wk", 2 * P, D),
-            4: (wq_raw, "wq", 0, 2 * P),
-            5: (wq_raw, "wq", 2 * P, D),
-        }
+        turn_steps = {}
+        quantise_steps = {}
+        for b in range(1, B):
+            first = (b - 1) * BLOCKS
+            for h, late in ((0, 0), (1, 1)) if b == 1 else ((0, 0), (1, 1)):
+                turn_steps[first + late] = turn_steps.get(first + late, []) + [(b, h)]
+            quantise_steps[first + (2 if b == 1 else 2)] = b
         for step in range(TILES + LAG_Q):
             if step < TILES:
                 stage_v(step)
+            if step == 0:
+                quantise_weight("wk", 128, 256)
+            if step == 1:
+                quantise_weight("wk", 256, 512)
+            if in_range(step - 0) and on_gpsimd(step - 0):
+                empty_k(step - 0)
+            if in_range(step - 1) and on_gpsimd(step - 1):
+                stage_score_gpsimd(step - 1)
             if in_range(step - LAG_SCORE) and not on_gpsimd(step - LAG_SCORE):
                 stage_score(step - LAG_SCORE)
-            if step in late_weights:
-                regroup_weight(nc.vector.tensor_copy, *late_weights[step])
             if in_range(step - LAG_MAX):
                 stage_max(step - LAG_MAX)
             if in_range(step - LAG_Q):
                 if step - LAG_Q == TILES - 1:
                     nc.vector.reciprocal(out=inv_denom[:], in_=denom[:])
                 stage_q(step - LAG_Q)
-            if step in late_weights:
-                quantise_weight(*late_weights[step][1:])
-            if step < TILES and on_gpsimd(step):
-                stage_score_gpsimd(step)
+            if step in quantise_steps:
+                quantise_x(quantise_steps[step])
             if in_range(step - LAG_K) and not on_gpsimd(step - LAG_K):
                 stage_k(step - LAG_K)
-            next_b = step // BLOCKS + 1
-            if next_b < B and step % BLOCKS == 2:
-                quantise_x(next_b)
-            if in_range(step - LAG_MAX):
-                stage_exp(step - LAG_MAX)
-            if next_b < B and step % BLOCKS < 2:
-                turn_x(next_b, step % BLOCKS)
-
+            if in_range(step - LAG_EXP):
+                stage_exp(step - LAG_EXP)
+            for b, h in turn_steps.get(step, []):
+                turn_x(b, h)
+                group_x(b, h)
+            if step == 1:
+                regroup_weight(nc.scalar.copy, wq_raw, "wq", 0, 128)
+            if step == 1:
+                regroup_weight(nc.scalar.copy, wq_raw, "wq", 128, 256)
+            if step == 2:
+                regroup_weight(nc.scalar.copy, wq_raw, "wq", 256, 384)
+            if step == 2:
+                regroup_weight(nc.scalar.copy, wq_raw, "wq", 384, 512)
+            if step == 2:
+                quantise_weight("wq", 0, 256)
+            if step == 3:
+                quantise_weight("wq", 256, 512)
 
         nc.vector.tensor_mul(out=result[:, 0:TILES], in0=numer[:], in1=inv_denom[:])
         result_ps = ps_misc.tile([P, P], F32, tag="misc", name="result_ps")

@@ -21,11 +21,11 @@ BLOCKS = S // P
 TILES = B * BLOCKS
 HALF_S = S // 2
 LAG_K = 1
-LAG_SCORE = 2
-LAG_MAX = 3
-LAG_EXP = 3
+LAG_SCORE = 3
+LAG_MAX = 4
+LAG_EXP = 4
 FUSED = 4
-LAG_Q = 5
+LAG_Q = 6
 
 FLOPS = 2 * B * S * E * 3 * D
 
@@ -197,7 +197,7 @@ def tile_multihead_attention_pa_t_kernel(tc, x, Wq, bq, Wk, bk, Wv, bv, out):
             return slice((t % BLOCKS) * P, (t % BLOCKS + 1) * P)
 
         def on_gpsimd(t):
-            return t % BLOCKS == BLOCKS - 1 and t >= BLOCKS
+            return t % BLOCKS == 1 and t >= BLOCKS
 
         v_biased = {}
         k_ps = {}

@@ -20,7 +20,7 @@ PACK = 4
 BLOCKS = S // P
 TILES = B * BLOCKS
 HALF_S = S // 2
-LAG_K = 1
+LAG_K = 2
 LAG_SCORE = 3
 LAG_MAX = 4
 LAG_EXP = 4
@@ -197,7 +197,7 @@ def tile_multihead_attention_pa_t_kernel(tc, x, Wq, bq, Wk, bk, Wv, bv, out):
             return slice((t % BLOCKS) * P, (t % BLOCKS + 1) * P)
 
         def on_gpsimd(t):
-            return t % BLOCKS == 1 and t >= BLOCKS
+            return t % BLOCKS == 2 and t >= BLOCKS
 
         v_biased = {}
         k_ps = {}
@@ -294,9 +294,9 @@ def tile_multihead_attention_pa_t_kernel(tc, x, Wq, bq, Wk, bk, Wv, bv, out):
         quantise_steps = {}
         for b in range(1, B):
             first = (b - 1) * BLOCKS
-            for h, late in ((0, 0), (1, 1)) if b == 1 else ((0, 0), (1, 1)):
+            for h, late in ((0, 1), (1, 2)) if b == 1 else ((0, 0), (1, 1)):
                 turn_steps[first + late] = turn_steps.get(first + late, []) + [(b, h)]
-            quantise_steps[first + (2 if b == 1 else 2)] = b
+            quantise_steps[first + (3 if b == 1 else 2)] = b
         for step in range(TILES + LAG_Q):
             if step < TILES:
                 stage_v(step)
@@ -325,17 +325,17 @@ def tile_multihead_attention_pa_t_kernel(tc, x, Wq, bq, Wk, bk, Wv, bv, out):
             for b, h in turn_steps.get(step, []):
                 turn_x(b, h)
                 group_x(b, h)
-            if step == 1:
+            if step == 0:
                 regroup_weight(nc.scalar.copy, wq_raw, "wq", 0, 128)
             if step == 1:
                 regroup_weight(nc.scalar.copy, wq_raw, "wq", 128, 256)
             if step == 2:
                 regroup_weight(nc.scalar.copy, wq_raw, "wq", 256, 384)
-            if step == 2:
-                regroup_weight(nc.scalar.copy, wq_raw, "wq", 384, 512)
-            if step == 2:
-                quantise_weight("wq", 0, 256)
             if step == 3:
+                regroup_weight(nc.scalar.copy, wq_raw, "wq", 384, 512)
+            if step == 4:
+                quantise_weight("wq", 0, 256)
+            if step == 5:
                 quantise_weight("wq", 256, 512)
 
         nc.vector.tensor_mul(out=result[:, 0:TILES], in0=numer[:], in1=inv_denom[:])

@@ -24,7 +24,7 @@ LAG_K = 2
 LAG_SCORE = 3
 LAG_MAX = 4
 LAG_EXP = 4
-FUSED = 4
+FUSED = 2
 LAG_Q = 6
 
 FLOPS = 2 * B * S * E * 3 * D
@@ -65,8 +65,8 @@ def tile_multihead_attention_pa_t_kernel(tc, x, Wq, bq, Wk, bk, Wv, bv, out):
             )
             return raw
 
-        wv_raw = load_weight(Wv, "wv")
         load_x(0, 0)
+        wv_raw = load_weight(Wv, "wv")
         load_x(0, 1)
         wk_raw = load_weight(Wk, "wk")
         load_x(1, 0)
@@ -88,12 +88,12 @@ def tile_multihead_attention_pa_t_kernel(tc, x, Wq, bq, Wk, bk, Wv, bv, out):
         nc.vector.memset(bias_rows[:], 0.0)
         bv_row = const.tile([P, D], BF16, name="bv_row")
         nc.vector.memset(bv_row[:], 0.0)
-        result = const.tile([P, P], F32, name="result")
-        nc.vector.memset(result[:], 0.0)
+        numer = const.tile([P, P], F32, name="numer")
+        nc.gpsimd.memset(numer[:], 0.0)
         neg_max = const.tile([P, TILES], F32, name="neg_max")
         denom = const.tile([P, TILES], F32, name="denom")
-        numer = const.tile([P, TILES], F32, name="numer")
-        inv_denom = const.tile([P, TILES], F32, name="inv_denom")
+        inv_denom = const.tile([P, P], F32, name="inv_denom")
+        nc.gpsimd.memset(inv_denom[:], 0.0)
 
         x_grouped = {}
         x_mx = {}
@@ -159,15 +159,15 @@ def tile_multihead_attention_pa_t_kernel(tc, x, Wq, bq, Wk, bk, Wv, bv, out):
 
         turn_x(0, 0)
         turn_x(0, 1)
-        regroup_weight(nc.scalar.copy, wv_raw, "wv", 0, 128)
         group_x(0, 0)
+        regroup_weight(nc.scalar.copy, wv_raw, "wv", 0, 128)
         group_x(0, 1)
         regroup_weight(nc.vector.tensor_copy, wv_raw, "wv", 128, 512)
         nc.vector.tensor_copy(out=bias_rows[0 : 2 * BLOCKS, :], in_=bias_in[:])
-        bias_ps = ps_misc.tile([P, P], F32, tag="misc", name="bias_ps")
+        bias_ps = ps_proj.tile([P, P], F32, tag="q", name="bias_ps")
         nc.tensor.transpose(bias_ps[:], bias_rows[:], ident[:])
         nc.vector.tensor_copy(out=bv_row[0:1, :], in_=bv_in[:])
-        bv_ps = ps_misc.tile([P, D], F32, tag="misc", name="bv_ps")
+        bv_ps = ps_proj.tile([P, D], F32, tag="q", name="bv_ps")
         nc.tensor.matmul(bv_ps[:], lhsT=ones[:], rhs=bv_row[:], start=True, stop=True)
         regroup_weight(nc.scalar.copy, wk_raw, "wk", 0, 128)
         bv_all = const.tile([P, D], F32, name="bv_all")
@@ -176,7 +176,8 @@ def tile_multihead_attention_pa_t_kernel(tc, x, Wq, bq, Wk, bk, Wv, bv, out):
         nc.scalar.copy(out=bias_cols[:], in_=bias_ps[:, 0 : 2 * BLOCKS])
         regroup_weight(nc.scalar.copy, wk_raw, "wk", 128, 256)
         quantise_weight("wv", 0, D)
-        quantise_x(0)
+        quantise_x(0, 0, HALF_S)
+        quantise_x(0, HALF_S, S)
         regroup_weight(nc.vector.tensor_copy, wk_raw, "wk", 256, 512)
         quantise_weight("wk", 0, P)
 
@@ -274,12 +275,16 @@ def tile_multihead_attention_pa_t_kernel(tc, x, Wq, bq, Wk, bk, Wv, bv, out):
                 accum_out=denom[:, t : t + 1],
             )
 
+        q_ps = {}
+
+        def multiply_q(t, tag="q"):
+            q_ps[t] = project(w_mx["wq"], block_cols(t), x_mx[t // BLOCKS], tag)
+
         def stage_q(t):
-            q_ps = project(w_mx["wq"], block_cols(t), x_mx[t // BLOCKS], "q")
             weighted = work.tile([P, S], F32, name="weighted")
             nc.vector.scalar_tensor_tensor(
                 out=weighted[:],
-                in0=q_ps[:],
+                in0=q_ps[t][:],
                 scalar=bias_cols[:, BLOCKS + t % BLOCKS : BLOCKS + t % BLOCKS + 1],
                 in1=weight[t][:],
                 op0=ALU.add,
@@ -294,7 +299,7 @@ def tile_multihead_attention_pa_t_kernel(tc, x, Wq, bq, Wk, bk, Wv, bv, out):
         quantise_steps = {}
         for b in range(1, B):
             first = (b - 1) * BLOCKS
-            for h, late in ((0, 1), (1, 2)) if b == 1 else ((0, 0), (1, 1)):
+            for h, late in ((0, 1), (1, 1)) if b == 1 else ((0, 0), (1, 1)):
                 turn_steps[first + late] = turn_steps.get(first + late, []) + [(b, h)]
             quantise_steps[first + (3 if b == 1 else 2)] = b
         for step in range(TILES + LAG_Q):
@@ -313,8 +318,17 @@ def tile_multihead_attention_pa_t_kernel(tc, x, Wq, bq, Wk, bk, Wv, bv, out):
             if in_range(step - LAG_MAX):
                 stage_max(step - LAG_MAX)
             if in_range(step - LAG_Q):
+                if step - LAG_Q < TILES - 2:
+                    multiply_q(step - LAG_Q)
+                if step - LAG_Q == TILES - 4:
+                    multiply_q(TILES - 2, "v")
+                    multiply_q(TILES - 1, "v")
                 if step - LAG_Q == TILES - 1:
-                    nc.vector.reciprocal(out=inv_denom[:], in_=denom[:])
+                    nc.vector.reciprocal(out=inv_denom[:, 0:TILES], in_=denom[:])
+                    inv_ps = ps_misc.tile([P, P], F32, tag="misc", name="inv_ps")
+                    nc.tensor.transpose(inv_ps[:], inv_denom[:], ident[:])
+                    inv_rows = const.tile([TILES, P], F32, name="inv_rows")
+                    nc.scalar.copy(out=inv_rows[:], in_=inv_ps[0:TILES, :])
                 stage_q(step - LAG_Q)
             if step in quantise_steps:
                 quantise_x(quantise_steps[step])
@@ -338,9 +352,8 @@ def tile_multihead_attention_pa_t_kernel(tc, x, Wq, bq, Wk, bk, Wv, bv, out):
             if step == 5:
                 quantise_weight("wq", 256, 512)
 
-        nc.vector.tensor_mul(out=result[:, 0:TILES], in0=numer[:], in1=inv_denom[:])
         result_ps = ps_misc.tile([P, P], F32, tag="misc", name="result_ps")
-        nc.tensor.transpose(result_ps[:], result[:], ident[:])
+        nc.tensor.transpose(result_ps[:], numer[:], ident[:])
         result_rows = const.tile([TILES, P], F32, name="result_rows")
-        nc.scalar.copy(out=result_rows[:], in_=result_ps[0:TILES, :])
+        nc.vector.tensor_mul(out=result_rows[:], in0=result_ps[0:TILES, :], in1=inv_rows[:])
         nc.sync.dma_start(out=out.rearrange("b h (r p) -> (b h r) p", p=P), in_=result_rows[:])

@@ -20,12 +20,12 @@ PACK = 4
 BLOCKS = S // P
 TILES = B * BLOCKS
 HALF_S = S // 2
-LAG_K = 2
-LAG_SCORE = 3
-LAG_MAX = 4
-LAG_EXP = 4
-FUSED = 2
-LAG_Q = 6
+LAG_K = 3
+LAG_SCORE = 4
+LAG_MAX = 5
+LAG_EXP = 5
+FUSED = 3
+LAG_Q = 7
 
 FLOPS = 2 * B * S * E * 3 * D
 
@@ -198,8 +198,9 @@ def tile_multihead_attention_pa_t_kernel(tc, x, Wq, bq, Wk, bk, Wv, bv, out):
             return slice((t % BLOCKS) * P, (t % BLOCKS + 1) * P)
 
         def on_gpsimd(t):
-            return t % BLOCKS == 2 and t >= BLOCKS
+            return t % 4 == 2 and t >= 4
 
+        v_sb = {}
         v_biased = {}
         k_ps = {}
         score = {}
@@ -207,8 +208,8 @@ def tile_multihead_attention_pa_t_kernel(tc, x, Wq, bq, Wk, bk, Wv, bv, out):
 
         def stage_v(t):
             v_ps = project(x_mx[t // BLOCKS], block_cols(t), w_mx["wv"], "v")
-            v_biased[t] = work.tile([P, S], F32, name="v_biased")
             if t < FUSED:
+                v_biased[t] = work.tile([P, S], F32, name="v_biased")
                 nc.vector.scalar_tensor_tensor(
                     out=v_biased[t][:],
                     in0=v_ps[:],
@@ -218,9 +219,28 @@ def tile_multihead_attention_pa_t_kernel(tc, x, Wq, bq, Wk, bk, Wv, bv, out):
                     op1=ALU.add,
                 )
             else:
-                v_sb = work.tile([P, S], F32, name="v_sb")
-                nc.scalar.mul(out=v_sb[:], in_=v_ps[:], mul=inv_sqrt_d)
-                nc.gpsimd.tensor_tensor(out=v_biased[t][:], in0=v_sb[:], in1=bv_all[:], op=ALU.add)
+                r = t % 4 - 1
+                merged = r in (0, 1) and t >= 4
+                if merged:
+                    if r == 0:
+                        v_sb[t] = work.tile([P, 2, S], F32, name="v_sb2")
+                        v_sb[t + 1] = v_sb[t]
+                    nc.scalar.mul(out=v_sb[t][:, r, :], in_=v_ps[:], mul=inv_sqrt_d)
+                    if r == 1:
+                        pair = work.tile([P, 2, S], F32, name="v_pair")
+                        nc.gpsimd.tensor_tensor(
+                            out=pair[:],
+                            in0=v_sb[t][:],
+                            in1=bv_all[:].unsqueeze(1).to_broadcast([P, 2, S]),
+                            op=ALU.add,
+                        )
+                        v_biased[t - 1] = pair[:, 0, :]
+                        v_biased[t] = pair[:, 1, :]
+                else:
+                    v_biased[t] = work.tile([P, S], F32, name="v_biased")
+                    v_sb1 = work.tile([P, S], F32, name="v_sb")
+                    nc.scalar.mul(out=v_sb1[:], in_=v_ps[:], mul=inv_sqrt_d)
+                    nc.gpsimd.tensor_tensor(out=v_biased[t][:], in0=v_sb1[:], in1=bv_all[:], op=ALU.add)
 
         def stage_k(t):
             k_ps[t] = project(w_mx["wk"], block_cols(t), x_mx[t // BLOCKS], "k")
@@ -311,8 +331,8 @@ def tile_multihead_attention_pa_t_kernel(tc, x, Wq, bq, Wk, bk, Wv, bv, out):
                 quantise_weight("wk", 256, 512)
             if in_range(step - 0) and on_gpsimd(step - 0):
                 empty_k(step - 0)
-            if in_range(step - 1) and on_gpsimd(step - 1):
-                stage_score_gpsimd(step - 1)
+            if in_range(step - 2) and on_gpsimd(step - 2):
+                stage_score_gpsimd(step - 2)
             if in_range(step - LAG_SCORE) and not on_gpsimd(step - LAG_SCORE):
                 stage_score(step - LAG_SCORE)
             if in_range(step - LAG_MAX):

@@ -296,20 +296,56 @@ def tile_multihead_attention_pa_t_kernel(tc, x, Wq, bq, Wk, bk, Wv, bv, out):
             )
 
         q_ps = {}
+        weighted = {}
+
+        def summed_on_scalar(t):
+            return t % BLOCKS == 0 and t < 26
 
         def multiply_q(t, tag="q"):
             q_ps[t] = project(w_mx["wq"], block_cols(t), x_mx[t // BLOCKS], tag)
 
         def stage_q(t):
-            weighted = work.tile([P, S], F32, name="weighted")
+            weighted[t] = work.tile([P, S], F32, name="weighted")
+            extra = {} if summed_on_scalar(t) else {"accum_out": numer[:, t : t + 1]}
             nc.vector.scalar_tensor_tensor(
-                out=weighted[:],
+                out=weighted[t][:],
                 in0=q_ps[t][:],
                 scalar=bias_cols[:, BLOCKS + t % BLOCKS : BLOCKS + t % BLOCKS + 1],
                 in1=weight[t][:],
                 op0=ALU.add,
                 op1=ALU.mult,
-                accum_out=numer[:, t : t + 1],
+                **extra,
+            )
+
+        def stage_sum(t):
+            nc.scalar.activation(
+                out=weighted[t][:], in_=weighted[t][:], func=ACT.Copy, accum_out=numer[:, t : t + 1]
+            )
+
+        LATE = (27, 28)
+        q_biased = {}
+        products = {}
+
+        def empty_q(t):
+            multiply_q(t, "v")
+            q_biased[t] = work.tile([P, S], F32, name="q_biased")
+            nc.scalar.activation(
+                out=q_biased[t][:],
+                in_=q_ps[t][:],
+                func=ACT.Identity,
+                bias=bias_cols[:, BLOCKS + t % BLOCKS : BLOCKS + t % BLOCKS + 1],
+                scale=1.0,
+            )
+
+        def multiply_weight(t):
+            products[t] = work.tile([P, S], F32, name="products")
+            nc.gpsimd.tensor_tensor(
+                out=products[t][:], in0=q_biased[t][:], in1=weight[t][:], op=ALU.mult
+            )
+
+        def sum_products(t):
+            nc.scalar.activation(
+                out=products[t][:], in_=products[t][:], func=ACT.Copy, accum_out=numer[:, t : t + 1]
             )
 
         def in_range(t):
@@ -337,12 +373,8 @@ def tile_multihead_attention_pa_t_kernel(tc, x, Wq, bq, Wk, bk, Wv, bv, out):
                 stage_score(step - LAG_SCORE)
             if in_range(step - LAG_MAX):
                 stage_max(step - LAG_MAX)
-            if in_range(step - LAG_Q):
-                if step - LAG_Q < TILES - 2:
-                    multiply_q(step - LAG_Q)
-                if step - LAG_Q == TILES - 4:
-                    multiply_q(TILES - 2, "v")
-                    multiply_q(TILES - 1, "v")
+            if in_range(step - LAG_Q) and step - LAG_Q not in LATE:
+                multiply_q(step - LAG_Q)
                 if step - LAG_Q == TILES - 1:
                     nc.vector.reciprocal(out=inv_denom[:, 0:TILES], in_=denom[:])
                     inv_ps = ps_misc.tile([P, P], F32, tag="misc", name="inv_ps")
@@ -354,8 +386,18 @@ def tile_multihead_attention_pa_t_kernel(tc, x, Wq, bq, Wk, bk, Wv, bv, out):
                 quantise_x(quantise_steps[step])
             if in_range(step - LAG_K) and not on_gpsimd(step - LAG_K):
                 stage_k(step - LAG_K)
+            for t in LATE:
+                if step == t + 5:
+                    empty_q(t)
             if in_range(step - LAG_EXP):
                 stage_exp(step - LAG_EXP)
+            for t in LATE:
+                if step == t + 6:
+                    multiply_weight(t)
+                if step == t + 9:
+                    sum_products(t)
+            if in_range(step - LAG_Q - 0) and summed_on_scalar(step - LAG_Q - 0):
+                stage_sum(step - LAG_Q - 0)
             for b, h in turn_steps.get(step, []):
                 turn_x(b, h)
                 group_x(b, h)
@@ -367,10 +409,8 @@ def tile_multihead_attention_pa_t_kernel(tc, x, Wq, bq, Wk, bk, Wv, bv, out):
                 regroup_weight(nc.scalar.copy, wq_raw, "wq", 256, 384)
             if step == 3:
                 regroup_weight(nc.scalar.copy, wq_raw, "wq", 384, 512)
-            if step == 4:
-                quantise_weight("wq", 0, 256)
             if step == 5:
-                quantise_weight("wq", 256, 512)
+                quantise_weight("wq", 0, 512)
 
         result_ps = ps_misc.tile([P, P], F32, tag="misc", name="result_ps")
         nc.tensor.transpose(result_ps[:], numer[:], ident[:])

@@ -299,7 +299,7 @@ def tile_multihead_attention_pa_t_kernel(tc, x, Wq, bq, Wk, bk, Wv, bv, out):
         weighted = {}
 
         def summed_on_scalar(t):
-            return t % BLOCKS == 0 and t < 26
+            return t % BLOCKS == 0 and t < 24
 
         def multiply_q(t, tag="q"):
             q_ps[t] = project(w_mx["wq"], block_cols(t), x_mx[t // BLOCKS], tag)
@@ -322,7 +322,7 @@ def tile_multihead_attention_pa_t_kernel(tc, x, Wq, bq, Wk, bk, Wv, bv, out):
                 out=weighted[t][:], in_=weighted[t][:], func=ACT.Copy, accum_out=numer[:, t : t + 1]
             )
 
-        LATE = (27, 28)
+        LATE = (26, 27)
         q_biased = {}
         products = {}
 
@@ -373,8 +373,12 @@ def tile_multihead_attention_pa_t_kernel(tc, x, Wq, bq, Wk, bk, Wv, bv, out):
                 stage_score(step - LAG_SCORE)
             if in_range(step - LAG_MAX):
                 stage_max(step - LAG_MAX)
+            if step == 35:
+                multiply_q(TILES - 2, "v")
+                multiply_q(TILES - 1, "v")
             if in_range(step - LAG_Q) and step - LAG_Q not in LATE:
-                multiply_q(step - LAG_Q)
+                if step - LAG_Q < TILES - 2:
+                    multiply_q(step - LAG_Q)
                 if step - LAG_Q == TILES - 1:
                     nc.vector.reciprocal(out=inv_denom[:, 0:TILES], in_=denom[:])
                     inv_ps = ps_misc.tile([P, P], F32, tag="misc", name="inv_ps")

@@ -41,18 +41,13 @@ def tile_multihead_attention_pa_t_kernel(tc, x, Wq, bq, Wk, bk, Wv, bv, out):
     ) as work, tc.psum_pool(name="ps_misc", bufs=2) as ps_misc, tc.psum_pool(
         name="ps_proj", bufs=2
     ) as ps_proj, tc.manual_schedule():
-        bias_in = const.tile([2 * BLOCKS, P], BF16, name="bias_in")
-        nc.scalar.dma_start(out=bias_in[0:BLOCKS, :], in_=bk.rearrange("(r c) -> r c", c=P))
-        nc.scalar.dma_start(out=bias_in[BLOCKS : 2 * BLOCKS, :], in_=bq.rearrange("(r c) -> r c", c=P))
-        bv_in = const.tile([1, D], BF16, name="bv_in")
-        nc.scalar.dma_start(out=bv_in[:], in_=bv.rearrange("(o n) -> o n", o=1))
-
         x_rows = {}
 
         def load_x(b, h):
             if h == 0:
                 x_rows[b] = xin.tile([P, BLOCKS * E], BF16, name="x_rows")
-            nc.sync.dma_start(
+            queue = nc.scalar if (b, h) == (0, 0) else nc.sync
+            queue.dma_start(
                 out=x_rows[b][:, h * 2 * E : (h + 1) * 2 * E].rearrange("p (r e) -> p r e", r=2),
                 in_=x[b, h * HALF_S : (h + 1) * HALF_S, :].rearrange("(r p) e -> p r e", p=P),
             )
@@ -66,6 +61,11 @@ def tile_multihead_attention_pa_t_kernel(tc, x, Wq, bq, Wk, bk, Wv, bv, out):
             return raw
 
         load_x(0, 0)
+        bias_in = const.tile([2 * BLOCKS, P], BF16, name="bias_in")
+        nc.sync.dma_start(out=bias_in[0:BLOCKS, :], in_=bk.rearrange("(r c) -> r c", c=P))
+        nc.sync.dma_start(out=bias_in[BLOCKS : 2 * BLOCKS, :], in_=bq.rearrange("(r c) -> r c", c=P))
+        bv_in = const.tile([1, D], BF16, name="bv_in")
+        nc.sync.dma_start(out=bv_in[:], in_=bv.rearrange("(o n) -> o n", o=1))
         wv_raw = load_weight(Wv, "wv")
         load_x(0, 1)
         wk_raw = load_weight(Wk, "wk")
@@ -157,18 +157,19 @@ def tile_multihead_attention_pa_t_kernel(tc, x, Wq, bq, Wk, bk, Wv, bv, out):
                 in_=w_grouped[name][:].rearrange("p n t -> p (n t)")[:, c0 * PACK : c1 * PACK],
             )
 
+        nc.vector.tensor_copy(out=bias_rows[0 : 2 * BLOCKS, :], in_=bias_in[:])
+        nc.vector.tensor_copy(out=bv_row[0:1, :], in_=bv_in[:])
+
         turn_x(0, 0)
+        bias_ps = ps_proj.tile([P, P], F32, tag="q", name="bias_ps")
+        nc.tensor.transpose(bias_ps[:], bias_rows[:], ident[:])
+        bv_ps = ps_proj.tile([P, D], F32, tag="q", name="bv_ps")
+        nc.tensor.matmul(bv_ps[:], lhsT=ones[:], rhs=bv_row[:], start=True, stop=True)
         turn_x(0, 1)
         group_x(0, 0)
         regroup_weight(nc.scalar.copy, wv_raw, "wv", 0, 128)
         group_x(0, 1)
         regroup_weight(nc.vector.tensor_copy, wv_raw, "wv", 128, 512)
-        nc.vector.tensor_copy(out=bias_rows[0 : 2 * BLOCKS, :], in_=bias_in[:])
-        bias_ps = ps_proj.tile([P, P], F32, tag="q", name="bias_ps")
-        nc.tensor.transpose(bias_ps[:], bias_rows[:], ident[:])
-        nc.vector.tensor_copy(out=bv_row[0:1, :], in_=bv_in[:])
-        bv_ps = ps_proj.tile([P, D], F32, tag="q", name="bv_ps")
-        nc.tensor.matmul(bv_ps[:], lhsT=ones[:], rhs=bv_row[:], start=True, stop=True)
         regroup_weight(nc.scalar.copy, wk_raw, "wk", 0, 128)
         bv_all = const.tile([P, D], F32, name="bv_all")
         nc.scalar.mul(out=bv_all[:], in_=bv_ps[:], mul=inv_sqrt_d)

@@ -157,6 +157,12 @@ def tile_multihead_attention_pa_t_kernel(tc, x, Wq, bq, Wk, bk, Wv, bv, out):
                 in_=w_grouped[name][:].rearrange("p n t -> p (n t)")[:, c0 * PACK : c1 * PACK],
             )
 
+        def copy_on_gpsimd(out, in_):
+            nc.gpsimd.tensor_scalar(out=out, in0=in_, scalar1=1.0, scalar2=0.0, op0=ALU.mult, op1=ALU.add)
+
+        SC = nc.scalar.copy
+        GC = copy_on_gpsimd
+        WQE = (GC, GC, SC, SC)
         nc.vector.tensor_copy(out=bias_rows[0 : 2 * BLOCKS, :], in_=bias_in[:])
         nc.vector.tensor_copy(out=bv_row[0:1, :], in_=bv_in[:])
 
@@ -406,14 +412,8 @@ def tile_multihead_attention_pa_t_kernel(tc, x, Wq, bq, Wk, bk, Wv, bv, out):
             for b, h in turn_steps.get(step, []):
                 turn_x(b, h)
                 group_x(b, h)
-            if step == 0:
-                regroup_weight(nc.scalar.copy, wq_raw, "wq", 0, 128)
-            if step == 1:
-                regroup_weight(nc.scalar.copy, wq_raw, "wq", 128, 256)
-            if step == 2:
-                regroup_weight(nc.scalar.copy, wq_raw, "wq", 256, 384)
-            if step == 3:
-                regroup_weight(nc.scalar.copy, wq_raw, "wq", 384, 512)
+            if step < 4:
+                regroup_weight(WQE[step], wq_raw, "wq", 128 * step, 128 * step + 128)
             if step == 5:
                 quantise_weight("wq", 0, 512)
 

import math

import concourse.mybir as mybir
from concourse.masks import make_identity

F32 = mybir.dt.float32
BF16 = mybir.dt.bfloat16
U32 = mybir.dt.uint32
U8 = mybir.dt.uint8
FP8X4 = mybir.dt.float8_e4m3fn_x4
ALU = mybir.AluOpType
ACT = mybir.ActivationFunctionType

B = 8
S = 512
E = 512
D = 512
P = 128
PACK = 4
BLOCKS = S // P
TILES = B * BLOCKS
HALF_S = S // 2
LAG_K = 3
LAG_SCORE = 4
LAG_MAX = 5
LAG_EXP = 5
FUSED = 3
LAG_Q = 7

FLOPS = 2 * B * S * E * 3 * D


def tile_multihead_attention_pa_t_kernel(tc, x, Wq, bq, Wk, bk, Wv, bv, out):
    nc = tc.nc
    inv_sqrt_d = 1.0 / math.sqrt(D)

    with tc.tile_pool(name="const", bufs=1) as const, tc.tile_pool(
        name="xin", bufs=B
    ) as xin, tc.tile_pool(name="xq", bufs=3) as xq, tc.tile_pool(
        name="work", bufs=6
    ) as work, tc.psum_pool(name="ps_misc", bufs=2) as ps_misc, tc.psum_pool(
        name="ps_proj", bufs=2
    ) as ps_proj, tc.manual_schedule():
        x_rows = {}

        def load_x(b, h):
            if h == 0:
                x_rows[b] = xin.tile([P, BLOCKS * E], BF16, name="x_rows")
            queue = nc.scalar if (b, h) == (0, 0) else nc.sync
            queue.dma_start(
                out=x_rows[b][:, h * 2 * E : (h + 1) * 2 * E].rearrange("p (r e) -> p r e", r=2),
                in_=x[b, h * HALF_S : (h + 1) * HALF_S, :].rearrange("(r p) e -> p r e", p=P),
            )

        def load_weight(w, name):
            raw = const.tile([P, PACK, D], BF16, name=name + "_raw")
            nc.sync.dma_start(
                out=raw[:].rearrange("p t n -> p (t n)"),
                in_=w.rearrange("(p t) n -> p (t n)", t=PACK),
            )
            return raw

        load_x(0, 0)
        bias_in = const.tile([2 * BLOCKS, P], BF16, name="bias_in")
        nc.sync.dma_start(out=bias_in[0:BLOCKS, :], in_=bk.rearrange("(r c) -> r c", c=P))
        nc.sync.dma_start(out=bias_in[BLOCKS : 2 * BLOCKS, :], in_=bq.rearrange("(r c) -> r c", c=P))
        bv_in = const.tile([1, D], BF16, name="bv_in")
        nc.sync.dma_start(out=bv_in[:], in_=bv.rearrange("(o n) -> o n", o=1))
        wv_raw = load_weight(Wv, "wv")
        load_x(0, 1)
        wk_raw = load_weight(Wk, "wk")
        load_x(1, 0)
        load_x(1, 1)
        wq_raw = load_weight(Wq, "wq")
        for b in range(2, B):
            load_x(b, 0)
            load_x(b, 1)

        ident = const.tile([P, P], F32, name="ident")
        make_identity(nc, ident[:])
        zero_col = const.tile([P, 1], F32, name="zero_col")
        nc.vector.memset(zero_col[:], 0.0)
        one_col = const.tile([P, 1], F32, name="one_col")
        nc.scalar.activation(out=one_col[:], in_=zero_col[:], func=ACT.Exp)
        ones = const.tile([P, P], BF16, name="ones")
        nc.vector.memset(ones[:], 1.0)
        bias_rows = const.tile([P, P], F32, name="bias_rows")
        nc.vector.memset(bias_rows[:], 0.0)
        bv_row = const.tile([P, D], BF16, name="bv_row")
        nc.vector.memset(bv_row[:], 0.0)
        numer = const.tile([P, P], F32, name="numer")
        nc.gpsimd.memset(numer[:], 0.0)
        neg_max = const.tile([P, TILES], F32, name="neg_max")
        denom = const.tile([P, TILES], F32, name="denom")
        inv_denom = const.tile([P, P], F32, name="inv_denom")
        nc.gpsimd.memset(inv_denom[:], 0.0)

        x_grouped = {}
        x_mx = {}

        x_turned = {}

        def turn_x(b, h):
            words = x_rows[b][:].bitcast(F32)
            xt = ps_misc.tile([P, 2, 2, P], F32, tag="misc", name="xt")
            for r in range(2):
                for u in range(2):
                    first = (2 * h + r) * (E // 2)
                    nc.tensor.transpose(
                        xt[:, r, u, :], words[:, first + u : first + E // 2 : 2], ident[:]
                    )
            x_turned[b, h] = xt

        def group_x(b, h):
            if h == 0:
                x_grouped[b] = xq.tile([P, S * PACK], BF16, name="x_grouped", align_bytes=64)
            nc.scalar.copy(
                out=x_grouped[b][:, h * HALF_S * PACK : (h + 1) * HALF_S * PACK]
                .bitcast(F32)
                .rearrange("p (r i u) -> p r i u", r=2, u=2),
                in_=x_turned[b, h][:].rearrange("p r u i -> p r i u"),
            )

        def quantise_x(b, c0=0, c1=S):
            if c0 == 0:
                x_mx[b] = (
                    xq.tile([P, S], U32, name="x_codes", align_bytes=64),
                    xq.tile([P, S], U8, name="x_scales", align_bytes=64),
                )
            codes, scales = x_mx[b]
            nc.vector.quantize_mx(
                out=codes[:, c0:c1].bitcast(FP8X4),
                scales=scales[:, c0:c1],
                in_=x_grouped[b][:, c0 * PACK : c1 * PACK],
            )

        w_grouped = {}
        w_mx = {}
        for name in ("wv", "wk", "wq"):
            w_grouped[name] = const.tile([P, D, PACK], BF16, name=name + "_grouped", align_bytes=64)
            w_mx[name] = (
                const.tile([P, D], U32, name=name + "_codes", align_bytes=64),
                const.tile([P, D], U8, name=name + "_scales", align_bytes=64),
            )

        def regroup_weight(copy, raw, name, c0, c1):
            copy(
                out=w_grouped[name][:, c0:c1, :].rearrange("p (c i) t -> p c t i", i=4),
                in_=raw[:, :, c0:c1].rearrange("p t (c i) -> p c t i", i=4),
            )

        def quantise_weight(name, c0, c1):
            codes, scales = w_mx[name]
            nc.vector.quantize_mx(
                out=codes[:, c0:c1].bitcast(FP8X4),
                scales=scales[:, c0:c1],
                in_=w_grouped[name][:].rearrange("p n t -> p (n t)")[:, c0 * PACK : c1 * PACK],
            )

        def copy_on_gpsimd(out, in_):
            nc.gpsimd.tensor_scalar(out=out, in0=in_, scalar1=1.0, scalar2=0.0, op0=ALU.mult, op1=ALU.add)

        SC = nc.scalar.copy
        GC = copy_on_gpsimd
        WQE = (GC, GC, SC, SC)
        nc.vector.tensor_copy(out=bias_rows[0 : 2 * BLOCKS, :], in_=bias_in[:])
        nc.vector.tensor_copy(out=bv_row[0:1, :], in_=bv_in[:])

        turn_x(0, 0)
        bias_ps = ps_proj.tile([P, P], F32, tag="q", name="bias_ps")
        nc.tensor.transpose(bias_ps[:], bias_rows[:], ident[:])
        bv_ps = ps_proj.tile([P, D], F32, tag="q", name="bv_ps")
        nc.tensor.matmul(bv_ps[:], lhsT=ones[:], rhs=bv_row[:], start=True, stop=True)
        turn_x(0, 1)
        group_x(0, 0)
        regroup_weight(nc.scalar.copy, wv_raw, "wv", 0, 128)
        group_x(0, 1)
        regroup_weight(nc.vector.tensor_copy, wv_raw, "wv", 128, 512)
        regroup_weight(nc.scalar.copy, wk_raw, "wk", 0, 128)
        bv_all = const.tile([P, D], F32, name="bv_all")
        nc.scalar.mul(out=bv_all[:], in_=bv_ps[:], mul=inv_sqrt_d)
        bias_cols = const.tile([P, 2 * BLOCKS], F32, name="bias_cols")
        nc.scalar.copy(out=bias_cols[:], in_=bias_ps[:, 0 : 2 * BLOCKS])
        regroup_weight(nc.scalar.copy, wk_raw, "wk", 128, 256)
        quantise_weight("wv", 0, D)
        quantise_x(0, 0, HALF_S)
        quantise_x(0, HALF_S, S)
        regroup_weight(nc.vector.tensor_copy, wk_raw, "wk", 256, 512)
        quantise_weight("wk", 0, P)

        def project(lhs, lhs_cols, rhs, tag):
            acc = ps_proj.tile([P, S], F32, tag=tag, name=tag + "_ps")
            nc.tensor.matmul_mx(
                out=acc[:],
                lhsT=lhs[0][:, lhs_cols].bitcast(FP8X4),
                lhsT_scale=lhs[1][:, lhs_cols],
                rhs=rhs[0][:].bitcast(FP8X4),
                rhs_scale=rhs[1][:],
                start=True,
                stop=True,
            )
            return acc

        def block_cols(t):
            return slice((t % BLOCKS) * P, (t % BLOCKS + 1) * P)

        def on_gpsimd(t):
            return t % 4 == 2 and t >= 4

        v_sb = {}
        v_biased = {}
        k_ps = {}
        score = {}
        weight = {}

        def stage_v(t):
            v_ps = project(x_mx[t // BLOCKS], block_cols(t), w_mx["wv"], "v")
            if t < FUSED:
                v_biased[t] = work.tile([P, S], F32, name="v_biased")
                nc.vector.scalar_tensor_tensor(
                    out=v_biased[t][:],
                    in0=v_ps[:],
                    scalar=inv_sqrt_d,
                    in1=bv_all[:],
                    op0=ALU.mult,
                    op1=ALU.add,
                )
            else:
                r = t % 4 - 1
                merged = r in (0, 1) and t >= 4
                if merged:
                    if r == 0:
                        v_sb[t] = work.tile([P, 2, S], F32, name="v_sb2")
                        v_sb[t + 1] = v_sb[t]
                    nc.scalar.mul(out=v_sb[t][:, r, :], in_=v_ps[:], mul=inv_sqrt_d)
                    if r == 1:
                        pair = work.tile([P, 2, S], F32, name="v_pair")
                        nc.gpsimd.tensor_tensor(
                            out=pair[:],
                            in0=v_sb[t][:],
                            in1=bv_all[:].unsqueeze(1).to_broadcast([P, 2, S]),
                            op=ALU.add,
                        )
                        v_biased[t - 1] = pair[:, 0, :]
                        v_biased[t] = pair[:, 1, :]
                else:
                    v_biased[t] = work.tile([P, S], F32, name="v_biased")
                    v_sb1 = work.tile([P, S], F32, name="v_sb")
                    nc.scalar.mul(out=v_sb1[:], in_=v_ps[:], mul=inv_sqrt_d)
                    nc.gpsimd.tensor_tensor(out=v_biased[t][:], in0=v_sb1[:], in1=bv_all[:], op=ALU.add)

        def stage_k(t):
            k_ps[t] = project(w_mx["wk"], block_cols(t), x_mx[t // BLOCKS], "k")

        k_biased = {}

        def empty_k(t):
            stage_k(t)
            k_biased[t] = work.tile([P, S], F32, name="k_biased")
            nc.scalar.activation(
                out=k_biased[t][:],
                in_=k_ps[t][:],
                func=ACT.Identity,
                bias=bias_cols[:, t % BLOCKS : t % BLOCKS + 1],
                scale=1.0,
            )

        def stage_score_gpsimd(t):
            score[t] = work.tile([P, S], F32, name="score")
            nc.gpsimd.tensor_tensor(
                out=score[t][:], in0=k_biased[t][:], in1=v_biased[t][:], op=ALU.mult
            )

        def stage_score(t):
            score[t] = work.tile([P, S], F32, name="score")
            nc.vector.scalar_tensor_tensor(
                out=score[t][:],
                in0=k_ps[t][:],
                scalar=bias_cols[:, t % BLOCKS : t % BLOCKS + 1],
                in1=v_biased[t][:],
                op0=ALU.add,
                op1=ALU.mult,
            )

        def stage_max(t):
            nc.vector.tensor_reduce(
                out=neg_max[:, t : t + 1],
                in_=score[t][:],
                axis=mybir.AxisListType.X,
                op=ALU.max,
                negate=True,
            )

        def stage_exp(t):
            weight[t] = work.tile([P, S], F32, name="weight")
            nc.scalar.activation(
                out=weight[t][:],
                in_=score[t][:],
                func=ACT.Exp,
                bias=neg_max[:, t : t + 1],
                scale=1.0,
                accum_out=denom[:, t : t + 1],
            )

        q_ps = {}
        weighted = {}

        def summed_on_scalar(t):
            return t % BLOCKS == 0 and t < 24

        def multiply_q(t, tag="q"):
            q_ps[t] = project(w_mx["wq"], block_cols(t), x_mx[t // BLOCKS], tag)

        def stage_q(t):
            weighted[t] = work.tile([P, S], F32, name="weighted")
            extra = {} if summed_on_scalar(t) else {"accum_out": numer[:, t : t + 1]}
            nc.vector.scalar_tensor_tensor(
                out=weighted[t][:],
                in0=q_ps[t][:],
                scalar=bias_cols[:, BLOCKS + t % BLOCKS : BLOCKS + t % BLOCKS + 1],
                in1=weight[t][:],
                op0=ALU.add,
                op1=ALU.mult,
                **extra,
            )

        def stage_sum(t):
            nc.scalar.activation(
                out=weighted[t][:], in_=weighted[t][:], func=ACT.Copy, accum_out=numer[:, t : t + 1]
            )

        LATE = (26, 27)
        q_biased = {}
        products = {}

        def empty_q(t):
            multiply_q(t, "v")
            q_biased[t] = work.tile([P, S], F32, name="q_biased")
            nc.scalar.activation(
                out=q_biased[t][:],
                in_=q_ps[t][:],
                func=ACT.Identity,
                bias=bias_cols[:, BLOCKS + t % BLOCKS : BLOCKS + t % BLOCKS + 1],
                scale=1.0,
            )

        def multiply_weight(t):
            products[t] = work.tile([P, S], F32, name="products")
            nc.gpsimd.tensor_tensor(
                out=products[t][:], in0=q_biased[t][:], in1=weight[t][:], op=ALU.mult
            )

        def sum_products(t):
            nc.scalar.activation(
                out=products[t][:], in_=products[t][:], func=ACT.Copy, accum_out=numer[:, t : t + 1]
            )

        def in_range(t):
            return 0 <= t < TILES

        turn_steps = {}
        quantise_steps = {}
        for b in range(1, B):
            first = (b - 1) * BLOCKS
            for h, late in ((0, 1), (1, 1)) if b == 1 else ((0, 0), (1, 1)):
                turn_steps[first + late] = turn_steps.get(first + late, []) + [(b, h)]
            quantise_steps[first + (3 if b == 1 else 2)] = b
        for step in range(TILES + LAG_Q):
            if step < TILES:
                stage_v(step)
            if step == 0:
                quantise_weight("wk", 128, 256)
            if step == 1:
                quantise_weight("wk", 256, 512)
            if in_range(step - 0) and on_gpsimd(step - 0):
                empty_k(step - 0)
            if in_range(step - 2) and on_gpsimd(step - 2):
                stage_score_gpsimd(step - 2)
            if in_range(step - LAG_SCORE) and not on_gpsimd(step - LAG_SCORE):
                stage_score(step - LAG_SCORE)
            if in_range(step - LAG_MAX):
                stage_max(step - LAG_MAX)
            if step == 35:
                multiply_q(TILES - 2, "v")
                multiply_q(TILES - 1, "v")
            if in_range(step - LAG_Q) and step - LAG_Q not in LATE:
                if step - LAG_Q < TILES - 2:
                    multiply_q(step - LAG_Q)
                if step - LAG_Q == TILES - 1:
                    nc.vector.reciprocal(out=inv_denom[:, 0:TILES], in_=denom[:])
                    inv_ps = ps_misc.tile([P, P], F32, tag="misc", name="inv_ps")
                    nc.tensor.transpose(inv_ps[:], inv_denom[:], ident[:])
                    inv_rows = const.tile([TILES, P], F32, name="inv_rows")
                    nc.scalar.copy(out=inv_rows[:], in_=inv_ps[0:TILES, :])
                stage_q(step - LAG_Q)
            if step in quantise_steps:
                quantise_x(quantise_steps[step])
            if in_range(step - LAG_K) and not on_gpsimd(step - LAG_K):
                stage_k(step - LAG_K)
            for t in LATE:
                if step == t + 5:
                    empty_q(t)
            if in_range(step - LAG_EXP):
                stage_exp(step - LAG_EXP)
            for t in LATE:
                if step == t + 6:
                    multiply_weight(t)
                if step == t + 9:
                    sum_products(t)
            if in_range(step - LAG_Q - 0) and summed_on_scalar(step - LAG_Q - 0):
                stage_sum(step - LAG_Q - 0)
            for b, h in turn_steps.get(step, []):
                turn_x(b, h)
                group_x(b, h)
            if step < 4:
                regroup_weight(WQE[step], wq_raw, "wq", 128 * step, 128 * step + 128)
            if step == 5:
                quantise_weight("wq", 0, 512)

        result_ps = ps_misc.tile([P, P], F32, tag="misc", name="result_ps")
        nc.tensor.transpose(result_ps[:], numer[:], ident[:])
        result_rows = const.tile([TILES, P], F32, name="result_rows")
        nc.vector.tensor_mul(out=result_rows[:], in0=result_ps[0:TILES, :], in1=inv_rows[:])
        nc.sync.dma_start(out=out.rearrange("b h (r p) -> (b h r) p", p=P), in_=result_rows[:])
